import numpy as np
import ml_dtypes


def mxq(x, axis, fmt="e4m3"):
    dtype, down = {"e4m3": (ml_dtypes.float8_e4m3fn, 7), "e5m2": (ml_dtypes.float8_e5m2, 14)}[fmt]
    v = np.moveaxis(np.asarray(x, np.float32).astype(ml_dtypes.bfloat16).astype(np.float64), axis, -1)
    blocks = v.reshape(v.shape[:-1] + (-1, 32))
    amax = np.abs(blocks).max(-1, keepdims=True)
    byte = np.maximum(np.where(amax > 0, np.frexp(amax)[1] - 1 + 127, 0) - down, 1)
    scale = np.exp2(byte - 127.0)
    codes = (blocks / scale).astype(np.float32).astype(dtype).astype(np.float64)
    return np.moveaxis((codes * scale).reshape(v.shape), -1, axis)


WIDE = False


def mx_kscale(k):
    if not WIDE:
        return np.ones(k)
    levels = np.array([10, -10, 5, -5, 0])
    if k % 512:
        return np.exp2(np.random.permutation(np.resize(levels, k // 32))).repeat(32)
    a = np.empty((k // 512, 16))
    for p in range(k // 512):
        a[p, :8] = np.random.permutation(np.resize(levels, 8))
        for g in range(8):
            far = levels[np.abs(levels - a[p, g]) >= 10]
            a[p, g + 8] = far[np.random.randint(len(far))]
    return np.exp2(a.ravel()).repeat(32)


BF16 = ml_dtypes.bfloat16


def bf(x):
    return np.asarray(x, np.float32).astype(BF16)


def f64(x):
    return np.asarray(x).astype(np.float64)


B, T, D, H, DH, F = 4, 1024, 1024, 4, 64, 4096
A = H * DH
EPS = 1e-6


def layer_norm(v, gain, bias):
    mu = v.mean(-1, keepdims=True)
    var = np.square(v - mu).mean(-1, keepdims=True)
    return (v - mu) * (1.0 / np.sqrt(var + EPS)) * gain + bias


def setup_inputs():
    s = mx_kscale(D)
    r = np.random.standard_normal
    return {"x": bf(r((B, T, D))),
            "ln1_gain": bf((1.0 + 0.1 * r(D)) * s),
            "ln1_bias": bf(0.1 * r(D) * s),
            "wq": bf(r((D, A)) / np.sqrt(D) / s[:, None]),
            "bq": bf(0.1 * r(A)),
            "wk": bf(r((D, A)) / np.sqrt(D) / s[:, None]),
            "bk": bf(0.1 * r(A)),
            "wv": bf(r((D, A)) / np.sqrt(D) / s[:, None]),
            "bv": bf(0.1 * r(A))}


def reference(x, ln1_gain, ln1_bias, wq, bq, wk, bk, wv, bv):
    h = layer_norm(f64(x), f64(ln1_gain), f64(ln1_bias))
    hq = mxq(h, 2, "e4m3")
    q = ((hq @ mxq(f64(wq), 0, "e4m3")) + f64(bq)).reshape(B, T, H, DH)
    k = ((hq @ mxq(f64(wk), 0, "e4m3")) + f64(bk)).reshape(B, T, H, DH)
    v = ((hq @ mxq(f64(wv), 0, "e4m3")) + f64(bv)).reshape(B, T, H, DH)
    return q, k, v

@@ -1,0 +1,316 @@
+from contextlib import ExitStack
+
+import concourse.mybir as mybir
+from concourse.masks import make_identity
+
+F32 = mybir.dt.float32
+BF16 = mybir.dt.bfloat16
+U32 = mybir.dt.uint32
+U8 = mybir.dt.uint8
+FP8X4 = mybir.dt.float8_e4m3fn_x4
+ALU = mybir.AluOpType
+ACT = mybir.ActivationFunctionType
+
+P = 128
+PACK = 4
+K_PASS = P * PACK
+TOKENS = 4 * 1024
+D = 1024
+C = 256
+EPS = 1e-6
+
+PASSES = D // K_PASS
+K_TILES = D // P
+A = 4
+GROUP = A * P
+GROUPS = TOKENS // GROUP
+BN_MAX = 512
+BANK = 512
+QK = slice(0, 2 * C)
+V = slice(2 * C, 3 * C)
+
+STEPS = 2 * GROUPS
+LAG_TRANSPOSE = 5
+LAG_QUANTISE = 8
+LAG_MULTIPLY = 9
+LAG_OUT = 10
+
+FLOPS = 2 * TOKENS * D * 3 * C
+
+
+def tile_swidtblock_pa_t_kernel(
+    tc, x, ln1_gain, ln1_bias, wq, bq, wk, bk, wv, bv, out_0, out_1, out_2
+):
+    nc = tc.nc
+    x_groups = x.flatten_outer_dims().rearrange("(s p a) d -> s p a d", p=P, a=A)
+    out_groups = [
+        o.rearrange("b t h e -> (b t) (h e)").rearrange("(s p a) c -> s p a c", p=P, a=A)
+        for o in (out_0, out_1, out_2)
+    ]
+
+    with ExitStack() as ctx:
+        const = ctx.enter_context(tc.tile_pool(name="const", bufs=1))
+        xpool = ctx.enter_context(tc.tile_pool(name="xpool", bufs=GROUPS))
+        small = ctx.enter_context(tc.tile_pool(name="small", bufs=4))
+        work2 = ctx.enter_context(tc.tile_pool(name="work2", bufs=2))
+        work3 = ctx.enter_context(tc.tile_pool(name="work3", bufs=3))
+        psum = ctx.enter_context(tc.psum_pool(name="psum", bufs=8))
+        ctx.enter_context(tc.manual_schedule())
+
+        x_tiles = []
+
+        def load_x(s):
+            x_sb = xpool.tile([P, A, D], BF16)
+            nc.sync.dma_start(out=x_sb[:], in_=x_groups[s])
+            x_tiles.append(x_sb)
+
+        load_x(0)
+        w_raw = const.tile([P, 3, PASSES, PACK, C], BF16)
+        for o, w in enumerate((wq, wk, wv)):
+            nc.sync.dma_start(
+                out=w_raw[:, o], in_=w.rearrange("(g p j) c -> p g j c", j=PACK, p=P)
+            )
+        for s in range(1, GROUPS):
+            load_x(s)
+
+        ident = const.tile([P, P], F32)
+        make_identity(nc, ident[:])
+        eps = const.tile([P, 1], F32)
+        nc.vector.memset(eps[:], EPS)
+        ones = const.tile([P, P], BF16)
+        nc.vector.memset(ones[:], 1.0)
+
+        gain_raw = const.tile([P, PASSES, PACK], BF16)
+        bias_raw = const.tile([P, PASSES, PACK], BF16)
+        for raw, vec in ((gain_raw, ln1_gain), (bias_raw, ln1_bias)):
+            nc.scalar.dma_start(out=raw[:], in_=vec.rearrange("(g p j) -> p g j", p=P, j=PACK))
+        bias_rows = const.tile([P, 3 * C], BF16)
+        nc.vector.memset(bias_rows[:], 0.0)
+        for o, b in enumerate((bq, bk, bv)):
+            nc.scalar.dma_start(
+                out=bias_rows[0:1, o * C : (o + 1) * C], in_=b.rearrange("(r c) -> r c", r=1)
+            )
+        ln_cols = const.tile([P, 2 * K_TILES], F32)
+        out_bias = const.tile([P, 3 * C], F32)
+        spread = {}
+
+        def spread_vectors():
+            for name, cols, width in (("qk", QK, 2 * C), ("v", V, C)):
+                bias_ps = psum.tile([P, BANK], F32, tag="bank")
+                nc.tensor.matmul(
+                    bias_ps[:, 0:width], lhsT=ones[:], rhs=bias_rows[:, cols], start=True, stop=True
+                )
+                spread[name] = bias_ps
+
+        def keep_spread_vectors():
+            for i, raw in enumerate((gain_raw, bias_raw)):
+                nc.vector.tensor_copy(
+                    out=ln_cols[:, i * K_TILES : (i + 1) * K_TILES],
+                    in_=raw[:].rearrange("p g j -> p (g j)"),
+                )
+            nc.vector.tensor_copy(out=out_bias[:, QK], in_=spread["qk"][:, 0 : 2 * C])
+            nc.vector.tensor_copy(out=out_bias[:, V], in_=spread["v"][:, 0:C])
+
+        w_grouped = const.tile([P, PASSES, 3 * C, PACK], BF16, align_bytes=64)
+        w_codes = const.tile([P, PASSES, 3 * C], U32, align_bytes=64)
+        w_scales = const.tile([P, PASSES, 3 * C], U8, align_bytes=64)
+
+        def regroup_weights():
+            for o in range(3):
+                for g in range(PASSES):
+                    dst = w_grouped[:, g, o * C : (o + 1) * C, :]
+                    src = w_raw[:, o, g].rearrange("p j c -> p c j")
+                    if g % 2 == 0:
+                        nc.scalar.copy(out=dst, in_=src)
+                    else:
+                        nc.gpsimd.tensor_scalar(
+                            out=dst, in0=src, scalar1=1.0, scalar2=0.0, op0=ALU.mult, op1=ALU.add
+                        )
+
+        def quantise_weights():
+            for g in range(PASSES):
+                for cols in (QK, V):
+                    nc.vector.quantize_mx(
+                        out=w_codes[:, g, cols].bitcast(FP8X4),
+                        scales=w_scales[:, g, cols],
+                        in_=w_grouped[:, g, cols, :].rearrange("p c j -> p (c j)"),
+                    )
+
+        stat_tiles = {}
+        n_tiles = {}
+        h_tiles = {}
+        code_tiles = {}
+        acc_tiles = {}
+        result_tiles = {}
+
+        def statistics(s, tiles):
+            if s not in stat_tiles:
+                stats = small.tile([P, A, D // BN_MAX, 6], F32)
+                mean_var = small.tile([P, A, 2], F32)
+                stat_tiles[s] = (stats, mean_var)
+            stats, mean_var = stat_tiles[s]
+            for a in tiles:
+                for half in range(D // BN_MAX):
+                    nc.vector.bn_stats(
+                        out=stats[:, a, half, :],
+                        in_=x_tiles[s][:, a, half * BN_MAX : (half + 1) * BN_MAX],
+                    )
+            for a in tiles:
+                nc.vector.bn_aggr(
+                    out=mean_var[:, a, :], in_=stats[:, a].rearrange("p h s -> p (h s)")
+                )
+
+        def standard_deviation(s):
+            std = small.tile([P, A], F32)
+            nc.scalar.activation(
+                out=std[:], in_=stat_tiles[s][1][:, :, 1], func=ACT.Sqrt, bias=eps[:, 0:1], scale=1.0
+            )
+            stat_tiles[s] = stat_tiles[s] + (std,)
+
+        def scale_and_shift(s):
+            mean_var = stat_tiles[s][1]
+            std = stat_tiles[s][2]
+            rstd = small.tile([P, A], F32)
+            nc.vector.reciprocal(out=rstd[:], in_=std[:])
+            shift = small.tile([P, A], F32)
+            nc.vector.scalar_tensor_tensor(
+                out=shift[:], in0=mean_var[:, :, 0], scalar=-1.0, in1=rstd[:],
+                op0=ALU.mult, op1=ALU.mult,
+            )
+            n_sb = work2.tile([P, A, D], F32)
+            n_tiles[s] = (n_sb, rstd, shift)
+
+        def n_view(tile, a):
+            return tile[:, a, :].rearrange("q (g j p) -> q g j p", j=PACK, p=P)
+
+        def x_view(tile, a):
+            return tile[:, a, :].rearrange("q (g p j) -> q g j p", j=PACK, p=P)
+
+        def normalise_on_gpsimd(s, tiles):
+            n_sb, rstd, shift = n_tiles[s]
+            for a in tiles:
+                nc.gpsimd.tensor_scalar(
+                    out=n_view(n_sb, a), in0=x_view(x_tiles[s], a),
+                    scalar1=rstd[:, a : a + 1], scalar2=shift[:, a : a + 1],
+                    op0=ALU.mult, op1=ALU.add,
+                )
+
+        def normalise_on_scalar(s, tiles):
+            n_sb, rstd, shift = n_tiles[s]
+            for a in tiles:
+                nc.scalar.activation(
+                    out=n_view(n_sb, a), in_=x_view(x_tiles[s], a), func=ACT.Identity,
+                    scale=rstd[:, a : a + 1], bias=shift[:, a : a + 1],
+                )
+
+        def transpose_and_scale(s, g):
+            n_sb = n_tiles[s][0]
+            if s not in h_tiles:
+                h_t = work2.tile([P, K_TILES, GROUP], BF16)
+                grouped = work3.tile([P, PASSES, GROUP, PACK], BF16, align_bytes=64)
+                h_tiles[s] = (h_t, grouped)
+            h_t, grouped = h_tiles[s]
+            for t in range(g * PACK, (g + 1) * PACK):
+                bank = psum.tile([P, BANK], F32, tag="bank")
+                for a in range(A):
+                    nc.tensor.transpose(
+                        bank[:, a * P : (a + 1) * P], n_sb[:, a, t * P : (t + 1) * P], ident[:]
+                    )
+                nc.scalar.activation(
+                    out=h_t[:, t, :], in_=bank[:], func=ACT.Identity,
+                    scale=ln_cols[:, t : t + 1], bias=ln_cols[:, K_TILES + t : K_TILES + t + 1],
+                )
+            nc.gpsimd.tensor_scalar(
+                out=grouped[:, g],
+                in0=h_t[:, g * PACK : (g + 1) * PACK, :].rearrange("p j c -> p c j"),
+                scalar1=1.0, scalar2=0.0, op0=ALU.mult, op1=ALU.add,
+            )
+
+        def quantise(s, g):
+            grouped = h_tiles[s][1]
+            if s not in code_tiles:
+                codes = work3.tile([P, PASSES, GROUP], U32, align_bytes=64)
+                scales = work3.tile([P, PASSES, GROUP], U8, align_bytes=64)
+                code_tiles[s] = (codes, scales)
+            codes, scales = code_tiles[s]
+            nc.vector.quantize_mx(
+                out=codes[:, g, :].bitcast(FP8X4),
+                scales=scales[:, g, :],
+                in_=grouped[:, g].rearrange("p c j -> p (c j)"),
+            )
+
+        def multiply(s, tiles):
+            codes, scales = code_tiles[s]
+            for a in tiles:
+                tokens = slice(a * P, (a + 1) * P)
+                acc_qk = psum.tile([P, BANK], F32, tag="bank")
+                acc_v = psum.tile([P, BANK], F32, tag="bank")
+                acc_tiles[(s, a)] = (acc_qk, acc_v)
+                for g in range(PASSES):
+                    for acc, cols, width in ((acc_qk, QK, 2 * C), (acc_v, V, C)):
+                        nc.tensor.matmul_mx(
+                            out=acc[:, 0:width],
+                            lhsT=codes[:, g, tokens].bitcast(FP8X4),
+                            lhsT_scale=scales[:, g, tokens],
+                            rhs=w_codes[:, g, cols].bitcast(FP8X4),
+                            rhs_scale=w_scales[:, g, cols],
+                            start=(g == 0),
+                            stop=(g == PASSES - 1),
+                        )
+
+        def add_bias(s, tiles):
+            if s not in result_tiles:
+                result = work2.tile([P, 3, A, C], F32)
+                result_tiles[s] = result
+            result = result_tiles[s]
+            for a in tiles:
+                acc_qk, acc_v = acc_tiles[(s, a)]
+                nc.vector.tensor_tensor(
+                    out=result[:, 0:2, a, :],
+                    in0=acc_qk[:].rearrange("p (o c) -> p o c", o=2),
+                    in1=out_bias[:, QK].rearrange("p (o c) -> p o c", o=2),
+                    op=ALU.add,
+                )
+                nc.vector.tensor_tensor(
+                    out=result[:, 2, a, :], in0=acc_v[:, 0:C], in1=out_bias[:, V], op=ALU.add
+                )
+
+        def store(s):
+            for o in range(3):
+                nc.sync.dma_start(out=out_groups[o][s], in_=result_tiles[s][:, o])
+
+        def half_of(i):
+            return i // 2, i % 2, (2 * (i % 2), 2 * (i % 2) + 1)
+
+        regroup_weights()
+        for u in range(STEPS + LAG_OUT):
+            if u == 2:
+                spread_vectors()
+            if u == 3:
+                keep_spread_vectors()
+            if u == LAG_QUANTISE:
+                quantise_weights()
+            if 0 <= u - LAG_QUANTISE < STEPS:
+                s, g, tiles = half_of(u - LAG_QUANTISE)
+                quantise(s, g)
+            if 0 <= u - LAG_TRANSPOSE < STEPS:
+                s, g, tiles = half_of(u - LAG_TRANSPOSE)
+                transpose_and_scale(s, g)
+            if 0 <= u - LAG_MULTIPLY < STEPS:
+                s, g, tiles = half_of(u - LAG_MULTIPLY)
+                multiply(s, tiles)
+            if 0 <= u - 3 < STEPS and (u - 3) % 2 == 0:
+                normalise_on_scalar((u - 3) // 2, (0, 2))
+            if 0 <= u - LAG_OUT < STEPS:
+                s, g, tiles = half_of(u - LAG_OUT)
+                add_bias(s, tiles)
+                if g == 1:
+                    store(s)
+            if u < STEPS:
+                s, g, tiles = half_of(u)
+                statistics(s, tiles)
+                if g == 1:
+                    standard_deviation(s)
+            if 0 <= u - 2 < STEPS and (u - 2) % 2 == 0:
+                scale_and_shift((u - 2) // 2)
+                normalise_on_gpsimd((u - 2) // 2, (1, 3))

@@ -18,22 +18,22 @@ TOKENS = 4 * 1024
 D = 1024
 C = 256
 EPS = 1e-6
+TINY = 2.0**-60
 
 PASSES = D // K_PASS
-K_TILES = D // P
+SLOTS = PASSES * PACK
 A = 4
 GROUP = A * P
 GROUPS = TOKENS // GROUP
+T2 = 2
+UNIT = T2 * P
+UNITS = TOKENS // UNIT
 BN_MAX = 512
 BANK = 512
 QK = slice(0, 2 * C)
 V = slice(2 * C, 3 * C)
-
-STEPS = 2 * GROUPS
-LAG_TRANSPOSE = 5
-LAG_QUANTISE = 8
-LAG_MULTIPLY = 9
-LAG_OUT = 10
+VECTOR_UNITS = 5
+W_ENGINES = "SGSGSG"
 
 FLOPS = 2 * TOKENS * D * 3 * C
 
@@ -51,81 +51,112 @@ def tile_swidtblock_pa_t_kernel(
     with ExitStack() as ctx:
         const = ctx.enter_context(tc.tile_pool(name="const", bufs=1))
         xpool = ctx.enter_context(tc.tile_pool(name="xpool", bufs=GROUPS))
-        small = ctx.enter_context(tc.tile_pool(name="small", bufs=4))
+        small = ctx.enter_context(tc.tile_pool(name="small", bufs=8))
         work2 = ctx.enter_context(tc.tile_pool(name="work2", bufs=2))
         work3 = ctx.enter_context(tc.tile_pool(name="work3", bufs=3))
-        psum = ctx.enter_context(tc.psum_pool(name="psum", bufs=8))
+        work4 = ctx.enter_context(tc.tile_pool(name="work4", bufs=4))
+        psum = ctx.enter_context(tc.psum_pool(name="psum", bufs=4))
         ctx.enter_context(tc.manual_schedule())
 
         x_tiles = []
 
-        def load_x(s):
+        def load_x(s, parts):
             x_sb = xpool.tile([P, A, D], BF16)
-            nc.sync.dma_start(out=x_sb[:], in_=x_groups[s])
+            step = A // parts
+            for a in range(0, A, step):
+                nc.sync.dma_start(out=x_sb[:, a : a + step], in_=x_groups[s, :, a : a + step])
             x_tiles.append(x_sb)
 
-        load_x(0)
+        load_x(0, A)
         w_raw = const.tile([P, 3, PASSES, PACK, C], BF16)
-        for o, w in enumerate((wq, wk, wv)):
-            nc.sync.dma_start(
-                out=w_raw[:, o], in_=w.rearrange("(g p j) c -> p g j c", j=PACK, p=P)
-            )
-        for s in range(1, GROUPS):
-            load_x(s)
 
-        ident = const.tile([P, P], F32)
-        make_identity(nc, ident[:])
+        def load_w(o):
+            nc.sync.dma_start(
+                out=w_raw[:, o], in_=(wq, wk, wv)[o].rearrange("(g p j) c -> p g j c", j=PACK, p=P)
+            )
+
+        load_w(0)
+        load_x(1, 2)
+        load_w(1)
+        load_w(2)
+        for s in range(2, GROUPS):
+            load_x(s, 1)
+
         eps = const.tile([P, 1], F32)
         nc.vector.memset(eps[:], EPS)
-        ones = const.tile([P, P], BF16)
-        nc.vector.memset(ones[:], 1.0)
-
+        warm = const.tile([P, 1], F32)
+        nc.scalar.activation(
+            out=warm[:], in_=eps[:], func=ACT.Abs_reciprocal_sqrt, bias=eps[:, 0:1], scale=1.0
+        )
         gain_raw = const.tile([P, PASSES, PACK], BF16)
         bias_raw = const.tile([P, PASSES, PACK], BF16)
         for raw, vec in ((gain_raw, ln1_gain), (bias_raw, ln1_bias)):
             nc.scalar.dma_start(out=raw[:], in_=vec.rearrange("(g p j) -> p g j", p=P, j=PACK))
         bias_rows = const.tile([P, 3 * C], BF16)
-        nc.vector.memset(bias_rows[:], 0.0)
+        nc.gpsimd.memset(bias_rows[:], 0.0)
         for o, b in enumerate((bq, bk, bv)):
             nc.scalar.dma_start(
                 out=bias_rows[0:1, o * C : (o + 1) * C], in_=b.rearrange("(r c) -> r c", r=1)
             )
-        ln_cols = const.tile([P, 2 * K_TILES], F32)
-        out_bias = const.tile([P, 3 * C], F32)
-        spread = {}
+        ident = const.tile([P, P], F32)
+        make_identity(nc, ident[:])
+        ones = const.tile([P, P], BF16)
+        nc.gpsimd.memset(ones[:], 1.0)
+        gain = const.tile([P, PASSES, PACK], F32)
+        size = const.tile([P, PASSES, PACK], F32)
+        quotient = const.tile([P, PASSES, PACK], F32)
+        quotients = const.tile([P, PASSES, PACK, P], F32)
+        out_bias_qk = const.tile([P, 2, C], F32)
+        out_bias_v = const.tile([P, 2, C], F32)
+
+        def divide_bias():
+            nc.vector.tensor_scalar(
+                out=size[:], in0=gain_raw[:], scalar1=-1.0, scalar2=0.0, op0=ALU.mult, op1=ALU.add
+            )
+            nc.vector.tensor_tensor(out=size[:], in0=size[:], in1=gain_raw[:], op=ALU.max)
+            nc.vector.tensor_scalar(
+                out=size[:], in0=size[:], scalar1=TINY, scalar2=TINY, op0=ALU.is_lt, op1=ALU.mult
+            )
+            nc.vector.tensor_tensor(out=gain[:], in0=size[:], in1=gain_raw[:], op=ALU.add)
+            nc.vector.reciprocal(out=size[:], in_=gain[:])
+            nc.vector.tensor_tensor(out=quotient[:], in0=size[:], in1=bias_raw[:], op=ALU.mult)
+
+        def spread_quotients():
+            for g in range(PASSES):
+                bank = psum.tile([P, PACK, P], F32, tag="bank")
+                for j in range(PACK):
+                    nc.tensor.transpose(
+                        bank[:, j], quotient[:, g, j : j + 1].to_broadcast([P, P]), ident[:]
+                    )
+                nc.scalar.copy(out=quotients[:, g], in_=bank[:])
 
         def spread_vectors():
-            for name, cols, width in (("qk", QK, 2 * C), ("v", V, C)):
-                bias_ps = psum.tile([P, BANK], F32, tag="bank")
+            spread_qk = psum.tile([P, BANK], F32, tag="bank")
+            spread_v = psum.tile([P, BANK], F32, tag="bank")
+            for bank, cols, width in ((spread_qk, QK, 2 * C), (spread_v, V, C)):
                 nc.tensor.matmul(
-                    bias_ps[:, 0:width], lhsT=ones[:], rhs=bias_rows[:, cols], start=True, stop=True
+                    bank[:, 0:width], lhsT=ones[:], rhs=bias_rows[:, cols], start=True, stop=True
                 )
-                spread[name] = bias_ps
-
-        def keep_spread_vectors():
-            for i, raw in enumerate((gain_raw, bias_raw)):
-                nc.vector.tensor_copy(
-                    out=ln_cols[:, i * K_TILES : (i + 1) * K_TILES],
-                    in_=raw[:].rearrange("p g j -> p (g j)"),
-                )
-            nc.vector.tensor_copy(out=out_bias[:, QK], in_=spread["qk"][:, 0 : 2 * C])
-            nc.vector.tensor_copy(out=out_bias[:, V], in_=spread["v"][:, 0:C])
+            nc.scalar.copy(out=out_bias_qk[:].rearrange("p o c -> p (o c)"), in_=spread_qk[:])
+            for i in range(2):
+                nc.scalar.copy(out=out_bias_v[:, i], in_=spread_v[:, 0:C])
 
         w_grouped = const.tile([P, PASSES, 3 * C, PACK], BF16, align_bytes=64)
         w_codes = const.tile([P, PASSES, 3 * C], U32, align_bytes=64)
         w_scales = const.tile([P, PASSES, 3 * C], U8, align_bytes=64)
 
-        def regroup_weights():
-            for o in range(3):
-                for g in range(PASSES):
-                    dst = w_grouped[:, g, o * C : (o + 1) * C, :]
-                    src = w_raw[:, o, g].rearrange("p j c -> p c j")
-                    if g % 2 == 0:
-                        nc.scalar.copy(out=dst, in_=src)
-                    else:
-                        nc.gpsimd.tensor_scalar(
-                            out=dst, in0=src, scalar1=1.0, scalar2=0.0, op0=ALU.mult, op1=ALU.add
-                        )
+        def regroup_weight(o):
+            for g in range(PASSES):
+                dst = w_grouped[:, g, o * C : (o + 1) * C, :]
+                src = w_raw[:, o, g].rearrange("p j c -> p c j")
+                if W_ENGINES[2 * o + g] == "S":
+                    nc.scalar.copy(out=dst, in_=src)
+                elif W_ENGINES[2 * o + g] == "V":
+                    nc.vector.tensor_copy(out=dst, in_=src)
+                else:
+                    nc.gpsimd.tensor_scalar(
+                        out=dst, in0=src, scalar1=1.0, scalar2=0.0, op0=ALU.mult, op1=ALU.add
+                    )
 
         def quantise_weights():
             for g in range(PASSES):
@@ -136,120 +167,127 @@ def tile_swidtblock_pa_t_kernel(
                         in_=w_grouped[:, g, cols, :].rearrange("p c j -> p (c j)"),
                     )
 
-        stat_tiles = {}
+        mean_tiles = {}
+        rstd_tiles = {}
         n_tiles = {}
-        h_tiles = {}
+        bank_tiles = {}
+        grouped_tiles = {}
         code_tiles = {}
         acc_tiles = {}
         result_tiles = {}
 
-        def statistics(s, tiles):
-            if s not in stat_tiles:
-                stats = small.tile([P, A, D // BN_MAX, 6], F32)
-                mean_var = small.tile([P, A, 2], F32)
-                stat_tiles[s] = (stats, mean_var)
-            stats, mean_var = stat_tiles[s]
-            for a in tiles:
+        def x_of(i, b):
+            return x_tiles[i // 2][:, T2 * (i % 2) + b, :]
+
+        def vector_statistics(i):
+            mean_var = small.tile([P, T2, 2], F32)
+            mean_tiles[i] = mean_var
+            stats = [None] * T2
+            for b in range(T2):
+                pair = small.tile([P, D // BN_MAX, 6], F32)
+                stats[b] = pair
                 for half in range(D // BN_MAX):
                     nc.vector.bn_stats(
-                        out=stats[:, a, half, :],
-                        in_=x_tiles[s][:, a, half * BN_MAX : (half + 1) * BN_MAX],
+                        out=pair[:, half, :], in_=x_of(i, b)[:, half * BN_MAX : (half + 1) * BN_MAX]
                     )
-            for a in tiles:
+            for b in range(T2):
                 nc.vector.bn_aggr(
-                    out=mean_var[:, a, :], in_=stats[:, a].rearrange("p h s -> p (h s)")
+                    out=mean_var[:, b, :], in_=stats[b][:].rearrange("p h s -> p (h s)")
                 )
 
-        def standard_deviation(s):
-            std = small.tile([P, A], F32)
+        def scalar_statistics(i):
+            mean_squares = small.tile([P, T2, 2], F32)
+            mean_tiles[i] = mean_squares
+            unread = work2.tile([P, D], BF16)
+            for b in range(T2):
+                nc.scalar.activation(
+                    out=unread[:], in_=x_of(i, b), func=ACT.Identity, scale=-1.0 / D,
+                    accum_out=mean_squares[:, b, 0:1],
+                )
+            for b in range(T2):
+                nc.scalar.activation(
+                    out=unread[:], in_=x_of(i, b), func=ACT.Square, scale=1.0,
+                    bias=mean_squares[:, b, 0:1], accum_out=mean_squares[:, b, 1:2],
+                )
+
+        def deviation(i):
+            rstd = small.tile([P, T2], F32)
+            shift = small.tile([P, T2], F32)
+            rstd_tiles[i] = (rstd, shift)
             nc.scalar.activation(
-                out=std[:], in_=stat_tiles[s][1][:, :, 1], func=ACT.Sqrt, bias=eps[:, 0:1], scale=1.0
+                out=rstd[:], in_=mean_tiles[i][:, :, 1], func=ACT.Abs_reciprocal_sqrt,
+                bias=eps[:, 0:1], scale=1.0 if i < VECTOR_UNITS else 1.0 / D,
             )
-            stat_tiles[s] = stat_tiles[s] + (std,)
-
-        def scale_and_shift(s):
-            mean_var = stat_tiles[s][1]
-            std = stat_tiles[s][2]
-            rstd = small.tile([P, A], F32)
-            nc.vector.reciprocal(out=rstd[:], in_=std[:])
-            shift = small.tile([P, A], F32)
-            nc.vector.scalar_tensor_tensor(
-                out=shift[:], in0=mean_var[:, :, 0], scalar=-1.0, in1=rstd[:],
-                op0=ALU.mult, op1=ALU.mult,
+            factor = rstd
+            if i < VECTOR_UNITS:
+                factor = small.tile([P, T2], F32)
+                nc.scalar.activation(out=factor[:], in_=rstd[:], func=ACT.Copy, scale=-1.0)
+            nc.gpsimd.tensor_tensor(
+                out=shift[:], in0=mean_tiles[i][:, :, 0], in1=factor[:], op=ALU.mult
             )
-            n_sb = work2.tile([P, A, D], F32)
-            n_tiles[s] = (n_sb, rstd, shift)
 
-        def n_view(tile, a):
-            return tile[:, a, :].rearrange("q (g j p) -> q g j p", j=PACK, p=P)
-
-        def x_view(tile, a):
-            return tile[:, a, :].rearrange("q (g p j) -> q g j p", j=PACK, p=P)
-
-        def normalise_on_gpsimd(s, tiles):
-            n_sb, rstd, shift = n_tiles[s]
-            for a in tiles:
+        def normalise(i):
+            n_sb = work4.tile([P, T2, PASSES, PACK, P], F32)
+            n_tiles[i] = n_sb
+            rstd, shift = rstd_tiles[i]
+            for b in range(T2):
                 nc.gpsimd.tensor_scalar(
-                    out=n_view(n_sb, a), in0=x_view(x_tiles[s], a),
-                    scalar1=rstd[:, a : a + 1], scalar2=shift[:, a : a + 1],
+                    out=n_sb[:, b], in0=x_of(i, b).rearrange("q (g p j) -> q g j p", j=PACK, p=P),
+                    scalar1=rstd[:, b : b + 1], scalar2=shift[:, b : b + 1],
                     op0=ALU.mult, op1=ALU.add,
                 )
 
-        def normalise_on_scalar(s, tiles):
-            n_sb, rstd, shift = n_tiles[s]
-            for a in tiles:
-                nc.scalar.activation(
-                    out=n_view(n_sb, a), in_=x_view(x_tiles[s], a), func=ACT.Identity,
-                    scale=rstd[:, a : a + 1], bias=shift[:, a : a + 1],
-                )
-
-        def transpose_and_scale(s, g):
-            n_sb = n_tiles[s][0]
-            if s not in h_tiles:
-                h_t = work2.tile([P, K_TILES, GROUP], BF16)
-                grouped = work3.tile([P, PASSES, GROUP, PACK], BF16, align_bytes=64)
-                h_tiles[s] = (h_t, grouped)
-            h_t, grouped = h_tiles[s]
-            for t in range(g * PACK, (g + 1) * PACK):
-                bank = psum.tile([P, BANK], F32, tag="bank")
-                for a in range(A):
-                    nc.tensor.transpose(
-                        bank[:, a * P : (a + 1) * P], n_sb[:, a, t * P : (t + 1) * P], ident[:]
-                    )
-                nc.scalar.activation(
-                    out=h_t[:, t, :], in_=bank[:], func=ACT.Identity,
-                    scale=ln_cols[:, t : t + 1], bias=ln_cols[:, K_TILES + t : K_TILES + t + 1],
-                )
-            nc.gpsimd.tensor_scalar(
-                out=grouped[:, g],
-                in0=h_t[:, g * PACK : (g + 1) * PACK, :].rearrange("p j c -> p c j"),
-                scalar1=1.0, scalar2=0.0, op0=ALU.mult, op1=ALU.add,
-            )
-
-        def quantise(s, g):
-            grouped = h_tiles[s][1]
-            if s not in code_tiles:
-                codes = work3.tile([P, PASSES, GROUP], U32, align_bytes=64)
-                scales = work3.tile([P, PASSES, GROUP], U8, align_bytes=64)
-                code_tiles[s] = (codes, scales)
-            codes, scales = code_tiles[s]
-            nc.vector.quantize_mx(
-                out=codes[:, g, :].bitcast(FP8X4),
-                scales=scales[:, g, :],
-                in_=grouped[:, g].rearrange("p c j -> p (c j)"),
-            )
-
-        def multiply(s, tiles):
-            codes, scales = code_tiles[s]
-            for a in tiles:
-                tokens = slice(a * P, (a + 1) * P)
-                acc_qk = psum.tile([P, BANK], F32, tag="bank")
-                acc_v = psum.tile([P, BANK], F32, tag="bank")
-                acc_tiles[(s, a)] = (acc_qk, acc_v)
+        def transpose(i):
+            n_sb = n_tiles[i]
+            for b in range(T2):
                 for g in range(PASSES):
-                    for acc, cols, width in ((acc_qk, QK, 2 * C), (acc_v, V, C)):
+                    bank = psum.tile([P, PACK, P], F32, tag="bank")
+                    bank_tiles[(i, b, g)] = bank
+                    for j in range(PACK):
+                        nc.tensor.matmul(
+                            bank[:, j], lhsT=n_sb[:, b, g, j], rhs=ident[:], is_transpose=True,
+                            start=True, stop=False,
+                        )
+                        nc.tensor.matmul(
+                            bank[:, j], lhsT=quotients[:, g, j], rhs=ident[:], is_transpose=True,
+                            start=False, stop=True,
+                        )
+
+        def scale(i):
+            grouped = work2.tile([P, PASSES, UNIT, PACK], BF16, align_bytes=64)
+            grouped_tiles[i] = grouped
+            for b in range(T2):
+                for g in range(PASSES):
+                    nc.vector.tensor_tensor(
+                        out=grouped[:, g, b * P : (b + 1) * P, :],
+                        in0=bank_tiles[(i, b, g)][:].rearrange("p j n -> p n j"),
+                        in1=gain[:, g].unsqueeze(1).to_broadcast([P, P, PACK]),
+                        op=ALU.mult,
+                    )
+
+        def quantise(i):
+            codes = work3.tile([P, PASSES, UNIT], U32, align_bytes=64)
+            scales = work3.tile([P, PASSES, UNIT], U8, align_bytes=64)
+            code_tiles[i] = (codes, scales)
+            nc.vector.quantize_mx(
+                out=codes[:].rearrange("p g n -> p (g n)").bitcast(FP8X4),
+                scales=scales[:].rearrange("p g n -> p (g n)"),
+                in_=grouped_tiles[i][:].rearrange("p g n j -> p (g n j)"),
+            )
+
+        def multiply(i):
+            codes, scales = code_tiles[i]
+            acc_v = psum.tile([P, T2, C], F32, tag="product")
+            acc_tiles[i] = [acc_v]
+            for b in range(T2):
+                tokens = slice(b * P, (b + 1) * P)
+                acc_qk = psum.tile([P, 2, C], F32, tag="product")
+                acc_tiles[i].append(acc_qk)
+                qk_out = acc_qk[:].rearrange("p o c -> p (o c)")
+                for g in range(PASSES):
+                    for out, cols in ((qk_out, QK), (acc_v[:, b], V)):
                         nc.tensor.matmul_mx(
-                            out=acc[:, 0:width],
+                            out=out,
                             lhsT=codes[:, g, tokens].bitcast(FP8X4),
                             lhsT_scale=scales[:, g, tokens],
                             rhs=w_codes[:, g, cols].bitcast(FP8X4),
@@ -258,59 +296,68 @@ def tile_swidtblock_pa_t_kernel(
                             stop=(g == PASSES - 1),
                         )
 
-        def add_bias(s, tiles):
-            if s not in result_tiles:
-                result = work2.tile([P, 3, A, C], F32)
-                result_tiles[s] = result
-            result = result_tiles[s]
-            for a in tiles:
-                acc_qk, acc_v = acc_tiles[(s, a)]
+        def add_bias(i):
+            result = work4.tile([P, 3, T2, C], F32)
+            result_tiles[i] = result
+            acc_v, *acc_qk = acc_tiles[i]
+            for b in range(T2):
                 nc.vector.tensor_tensor(
-                    out=result[:, 0:2, a, :],
-                    in0=acc_qk[:].rearrange("p (o c) -> p o c", o=2),
-                    in1=out_bias[:, QK].rearrange("p (o c) -> p o c", o=2),
-                    op=ALU.add,
+                    out=result[:, 0:2, b, :], in0=acc_qk[b][:], in1=out_bias_qk[:], op=ALU.add
                 )
-                nc.vector.tensor_tensor(
-                    out=result[:, 2, a, :], in0=acc_v[:, 0:C], in1=out_bias[:, V], op=ALU.add
-                )
+            nc.vector.tensor_tensor(
+                out=result[:, 2], in0=acc_v[:], in1=out_bias_v[:], op=ALU.add
+            )
 
-        def store(s):
+        def store(i):
+            a = T2 * (i % 2)
             for o in range(3):
-                nc.sync.dma_start(out=out_groups[o][s], in_=result_tiles[s][:, o])
+                nc.sync.dma_start(
+                    out=out_groups[o][i // 2, :, a : a + T2], in_=result_tiles[i][:, o]
+                )
 
-        def half_of(i):
-            return i // 2, i % 2, (2 * (i % 2), 2 * (i % 2) + 1)
+        def stage(function, i):
+            if 0 <= i < UNITS:
+                function(i)
 
-        regroup_weights()
-        for u in range(STEPS + LAG_OUT):
-            if u == 2:
-                spread_vectors()
-            if u == 3:
-                keep_spread_vectors()
-            if u == LAG_QUANTISE:
+        def scalar_front(i):
+            if i >= VECTOR_UNITS:
+                scalar_statistics(i)
+                deviation(i)
+
+        def front(i):
+            if i < VECTOR_UNITS:
+                vector_statistics(i)
+            else:
+                scalar_statistics(i)
+
+        front(0)
+        deviation(0)
+        normalise(0)
+        divide_bias()
+        spread_quotients()
+        transpose(0)
+        front(1)
+        deviation(1)
+        normalise(1)
+        regroup_weight(0)
+        front(2)
+        spread_vectors()
+        deviation(2)
+        normalise(2)
+        regroup_weight(1)
+        regroup_weight(2)
+        front(3)
+        deviation(3)
+        front(4)
+        for u in range(UNITS + 3):
+            stage(front, u + 5)
+            stage(deviation, u + 4)
+            stage(normalise, u + 3)
+            stage(scale, u)
+            stage(multiply, u - 2)
+            stage(transpose, u + 1)
+            if u == 1:
                 quantise_weights()
-            if 0 <= u - LAG_QUANTISE < STEPS:
-                s, g, tiles = half_of(u - LAG_QUANTISE)
-                quantise(s, g)
-            if 0 <= u - LAG_TRANSPOSE < STEPS:
-                s, g, tiles = half_of(u - LAG_TRANSPOSE)
-                transpose_and_scale(s, g)
-            if 0 <= u - LAG_MULTIPLY < STEPS:
-                s, g, tiles = half_of(u - LAG_MULTIPLY)
-                multiply(s, tiles)
-            if 0 <= u - 3 < STEPS and (u - 3) % 2 == 0:
-                normalise_on_scalar((u - 3) // 2, (0, 2))
-            if 0 <= u - LAG_OUT < STEPS:
-                s, g, tiles = half_of(u - LAG_OUT)
-                add_bias(s, tiles)
-                if g == 1:
-                    store(s)
-            if u < STEPS:
-                s, g, tiles = half_of(u)
-                statistics(s, tiles)
-                if g == 1:
-                    standard_deviation(s)
-            if 0 <= u - 2 < STEPS and (u - 2) % 2 == 0:
-                scale_and_shift((u - 2) // 2)
-                normalise_on_gpsimd((u - 2) // 2, (1, 3))
+            stage(add_bias, u - 2)
+            stage(store, u - 2)
+            stage(quantise, u)

@@ -32,8 +32,9 @@ BN_MAX = 512
 BANK = 512
 QK = slice(0, 2 * C)
 V = slice(2 * C, 3 * C)
-VECTOR_UNITS = 5
-W_ENGINES = "SGSGSG"
+VECTOR_UNITS = 2
+SCALAR_UNITS = 2
+W_ENGINES = "GGGGGG"
 
 FLOPS = 2 * TOKENS * D * 3 * C
 
@@ -56,7 +57,6 @@ def tile_swidtblock_pa_t_kernel(
         work3 = ctx.enter_context(tc.tile_pool(name="work3", bufs=3))
         work4 = ctx.enter_context(tc.tile_pool(name="work4", bufs=4))
         psum = ctx.enter_context(tc.psum_pool(name="psum", bufs=4))
-        ctx.enter_context(tc.manual_schedule())
 
         x_tiles = []
 
@@ -90,6 +90,7 @@ def tile_swidtblock_pa_t_kernel(
         )
         gain_raw = const.tile([P, PASSES, PACK], BF16)
         bias_raw = const.tile([P, PASSES, PACK], BF16)
+        bias = const.tile([P, PASSES, PACK], F32)
         for raw, vec in ((gain_raw, ln1_gain), (bias_raw, ln1_bias)):
             nc.scalar.dma_start(out=raw[:], in_=vec.rearrange("(g p j) -> p g j", p=P, j=PACK))
         bias_rows = const.tile([P, 3 * C], BF16)
@@ -118,6 +119,7 @@ def tile_swidtblock_pa_t_kernel(
                 out=size[:], in0=size[:], scalar1=TINY, scalar2=TINY, op0=ALU.is_lt, op1=ALU.mult
             )
             nc.vector.tensor_tensor(out=gain[:], in0=size[:], in1=gain_raw[:], op=ALU.add)
+            nc.scalar.copy(out=bias[:], in_=bias_raw[:])
             nc.vector.reciprocal(out=size[:], in_=gain[:])
             nc.vector.tensor_tensor(out=quotient[:], in0=size[:], in1=bias_raw[:], op=ALU.mult)
 
@@ -230,14 +232,46 @@ def tile_swidtblock_pa_t_kernel(
             n_sb = work4.tile([P, T2, PASSES, PACK, P], F32)
             n_tiles[i] = n_sb
             rstd, shift = rstd_tiles[i]
+            engine = nc.vector if i < VECTOR_UNITS else nc.gpsimd
             for b in range(T2):
-                nc.gpsimd.tensor_scalar(
+                engine.tensor_scalar(
                     out=n_sb[:, b], in0=x_of(i, b).rearrange("q (g p j) -> q g j p", j=PACK, p=P),
                     scalar1=rstd[:, b : b + 1], scalar2=shift[:, b : b + 1],
                     op0=ALU.mult, op1=ALU.add,
                 )
 
+        def transpose_alone(i):
+            n_sb = n_tiles[i]
+            for g in range(PASSES):
+                for half in range(2):
+                    bank = psum.tile([P, 2, UNIT], F32, tag="bank")
+                    bank_tiles[(i, g, half)] = bank
+                    for jj in range(2):
+                        for b in range(T2):
+                            nc.tensor.transpose(
+                                bank[:, jj, b * P : (b + 1) * P], n_sb[:, b, g, 2 * half + jj],
+                                ident[:],
+                            )
+
+        def scale_on_scalar(i):
+            grouped = work2.tile([P, PASSES, UNIT, PACK], BF16, align_bytes=64)
+            grouped_tiles[i] = grouped
+            for g in range(PASSES):
+                h_t = work2.tile([P, PACK, UNIT], BF16)
+                for j in range(PACK):
+                    nc.scalar.activation(
+                        out=h_t[:, j], in_=bank_tiles[(i, g, j // 2)][:, j % 2], func=ACT.Identity,
+                        scale=gain[:, g, j : j + 1], bias=bias[:, g, j : j + 1],
+                    )
+                nc.gpsimd.tensor_scalar(
+                    out=grouped[:, g], in0=h_t[:].rearrange("p j c -> p c j"),
+                    scalar1=1.0, scalar2=0.0, op0=ALU.mult, op1=ALU.add,
+                )
+
         def transpose(i):
+            if i >= UNITS - SCALAR_UNITS:
+                transpose_alone(i)
+                return
             n_sb = n_tiles[i]
             for b in range(T2):
                 for g in range(PASSES):
@@ -254,6 +288,9 @@ def tile_swidtblock_pa_t_kernel(
                         )
 
         def scale(i):
+            if i >= UNITS - SCALAR_UNITS:
+                scale_on_scalar(i)
+                return
             grouped = work2.tile([P, PASSES, UNIT, PACK], BF16, align_bytes=64)
             grouped_tiles[i] = grouped
             for b in range(T2):
@@ -339,15 +376,14 @@ def tile_swidtblock_pa_t_kernel(
         front(1)
         deviation(1)
         normalise(1)
-        regroup_weight(0)
+        for o in range(3):
+            regroup_weight(o)
         front(2)
-        spread_vectors()
         deviation(2)
         normalise(2)
-        regroup_weight(1)
-        regroup_weight(2)
         front(3)
         deviation(3)
+        spread_vectors()
         front(4)
         for u in range(UNITS + 3):
             stage(front, u + 5)

@@ -32,7 +32,8 @@ BN_MAX = 512
 BANK = 512
 QK = slice(0, 2 * C)
 V = slice(2 * C, 3 * C)
-VECTOR_UNITS = 2
+S_EXTRA = ()
+VECTOR_UNITS = 3
 SCALAR_UNITS = 2
 W_ENGINES = "GGGGGG"
 
@@ -57,6 +58,8 @@ def tile_swidtblock_pa_t_kernel(
         work3 = ctx.enter_context(tc.tile_pool(name="work3", bufs=3))
         work4 = ctx.enter_context(tc.tile_pool(name="work4", bufs=4))
         psum = ctx.enter_context(tc.psum_pool(name="psum", bufs=4))
+
+        ctx.enter_context(tc.manual_schedule(engines={mybir.EngineType.DVE}))
 
         x_tiles = []
 
@@ -186,6 +189,9 @@ def tile_swidtblock_pa_t_kernel(
             mean_tiles[i] = mean_var
             stats = [None] * T2
             for b in range(T2):
+                if (i, b) in S_EXTRA:
+                    scalar_tile(i, b)
+                    continue
                 pair = small.tile([P, D // BN_MAX, 6], F32)
                 stats[b] = pair
                 for half in range(D // BN_MAX):
@@ -193,9 +199,27 @@ def tile_swidtblock_pa_t_kernel(
                         out=pair[:, half, :], in_=x_of(i, b)[:, half * BN_MAX : (half + 1) * BN_MAX]
                     )
             for b in range(T2):
+                if (i, b) in S_EXTRA:
+                    continue
                 nc.vector.bn_aggr(
                     out=mean_var[:, b, :], in_=stats[b][:].rearrange("p h s -> p (h s)")
                 )
+
+        def scalar_tile(i, b):
+            mean_var = mean_tiles[i]
+            unread = work2.tile([P, D], BF16)
+            squares = small.tile([P, 1], F32)
+            nc.scalar.activation(
+                out=unread[:], in_=x_of(i, b), func=ACT.Identity, scale=1.0 / D,
+                accum_out=mean_var[:, b, 0:1],
+            )
+            nc.scalar.activation(
+                out=unread[:], in_=x_of(i, b), func=ACT.Square, scale=-1.0,
+                bias=mean_var[:, b, 0:1], accum_out=squares[:],
+            )
+            nc.scalar.activation(
+                out=mean_var[:, b, 1:2], in_=squares[:], func=ACT.Copy, scale=1.0 / D
+            )
 
         def scalar_statistics(i):
             mean_squares = small.tile([P, T2, 2], F32)
@@ -220,19 +244,19 @@ def tile_swidtblock_pa_t_kernel(
                 out=rstd[:], in_=mean_tiles[i][:, :, 1], func=ACT.Abs_reciprocal_sqrt,
                 bias=eps[:, 0:1], scale=1.0 if i < VECTOR_UNITS else 1.0 / D,
             )
-            factor = rstd
-            if i < VECTOR_UNITS:
-                factor = small.tile([P, T2], F32)
-                nc.scalar.activation(out=factor[:], in_=rstd[:], func=ACT.Copy, scale=-1.0)
-            nc.gpsimd.tensor_tensor(
-                out=shift[:], in0=mean_tiles[i][:, :, 0], in1=factor[:], op=ALU.mult
+
+        def shift_of(i):
+            rstd, shift = rstd_tiles[i]
+            nc.vector.scalar_tensor_tensor(
+                out=shift[:], in0=mean_tiles[i][:, :, 0], scalar=-1.0 if i < VECTOR_UNITS else 1.0,
+                in1=rstd[:], op0=ALU.mult, op1=ALU.mult,
             )
 
         def normalise(i):
             n_sb = work4.tile([P, T2, PASSES, PACK, P], F32)
             n_tiles[i] = n_sb
             rstd, shift = rstd_tiles[i]
-            engine = nc.vector if i < VECTOR_UNITS else nc.gpsimd
+            engine = nc.vector if i < 1 else nc.gpsimd
             for b in range(T2):
                 engine.tensor_scalar(
                     out=n_sb[:, b], in0=x_of(i, b).rearrange("q (g p j) -> q g j p", j=PACK, p=P),
@@ -269,7 +293,7 @@ def tile_swidtblock_pa_t_kernel(
                 )
 
         def transpose(i):
-            if i >= UNITS - SCALAR_UNITS:
+            if i in (14, 15):
                 transpose_alone(i)
                 return
             n_sb = n_tiles[i]
@@ -288,7 +312,7 @@ def tile_swidtblock_pa_t_kernel(
                         )
 
         def scale(i):
-            if i >= UNITS - SCALAR_UNITS:
+            if i in (14, 15):
                 scale_on_scalar(i)
                 return
             grouped = work2.tile([P, PASSES, UNIT, PACK], BF16, align_bytes=64)
@@ -369,31 +393,43 @@ def tile_swidtblock_pa_t_kernel(
 
         front(0)
         deviation(0)
-        normalise(0)
         divide_bias()
+        shift_of(0)
+        normalise(0)
         spread_quotients()
         transpose(0)
         front(1)
         deviation(1)
+        regroup_weight(0)
+        shift_of(1)
         normalise(1)
-        for o in range(3):
-            regroup_weight(o)
+        regroup_weight(1)
+        regroup_weight(2)
         front(2)
         deviation(2)
+        scale(0)
+        shift_of(2)
         normalise(2)
+        transpose(1)
         front(3)
         deviation(3)
         spread_vectors()
+        quantise(0)
         front(4)
-        for u in range(UNITS + 3):
-            stage(front, u + 5)
-            stage(deviation, u + 4)
-            stage(normalise, u + 3)
+        scale(1)
+        shift_of(3)
+        normalise(3)
+        quantise_weights()
+        transpose(2)
+        quantise(1)
+        for u in range(2, UNITS + 3):
+            stage(front, u + 3)
+            stage(deviation, u + 2)
+            stage(shift_of, u + 2)
+            stage(normalise, u + 2)
             stage(scale, u)
             stage(multiply, u - 2)
             stage(transpose, u + 1)
-            if u == 1:
-                quantise_weights()
             stage(add_bias, u - 2)
             stage(store, u - 2)
             stage(quantise, u)

@@ -126,8 +126,30 @@ def tile_swidtblock_pa_t_kernel(
             nc.vector.reciprocal(out=size[:], in_=gain[:])
             nc.vector.tensor_tensor(out=quotient[:], in0=size[:], in1=bias_raw[:], op=ALU.mult)
 
+        parts = const.tile([P, PACK, P // PACK], F32)
+        nc.gpsimd.memset(parts[:], 0.0)
+        rest = const.tile([P, PACK], F32)
+        rounded = const.tile([P, 2, PACK], BF16)
+        parts_by_row = const.tile([P, P], BF16)
+        selector = const.tile([P, PACK, P], BF16)
+        nc.gpsimd.memset(selector[:], 0.0)
+        for j in range(PACK):
+            nc.gpsimd.memset(selector[32 * j : 32 * (j + 1), j], 1.0)
+
+        def split_quotients():
+            left = quotient[:, 0]
+            for i in range(2):
+                nc.scalar.copy(out=rounded[:, i], in_=left)
+                nc.scalar.copy(out=parts[:, :, i], in_=rounded[:, i])
+                out = rest[:] if i == 0 else parts[:, :, 2]
+                nc.vector.tensor_tensor(out=out, in0=left, in1=rounded[:, i], op=ALU.subtract)
+                left = rest[:]
+            bank = psum.tile([P, PACK, P], F32, tag="bank")
+            nc.tensor.transpose(bank[:, 0], parts[:].rearrange("p j i -> p (j i)"), ident[:])
+            nc.scalar.copy(out=parts_by_row[:], in_=bank[:, 0])
+
         def spread_quotients():
-            for g in range(PASSES):
+            for g in range(1, PASSES):
                 bank = psum.tile([P, PACK, P], F32, tag="bank")
                 for j in range(PACK):
                     nc.tensor.transpose(
@@ -301,6 +323,17 @@ def tile_swidtblock_pa_t_kernel(
                 for g in range(PASSES):
                     bank = psum.tile([P, PACK, P], F32, tag="bank")
                     bank_tiles[(i, b, g)] = bank
+                    if g == 0:
+                        nc.tensor.matmul(
+                            bank[:].rearrange("p j n -> p (j n)"), lhsT=parts_by_row[:],
+                            rhs=selector[:].rearrange("p j n -> p (j n)"), start=True, stop=False,
+                        )
+                        for j in range(PACK):
+                            nc.tensor.matmul(
+                                bank[:, j], lhsT=n_sb[:, b, g, j], rhs=ident[:], is_transpose=True,
+                                start=False, stop=(j == PACK - 1),
+                            )
+                        continue
                     for j in range(PACK):
                         nc.tensor.matmul(
                             bank[:, j], lhsT=n_sb[:, b, g, j], rhs=ident[:], is_transpose=True,
@@ -396,6 +429,7 @@ def tile_swidtblock_pa_t_kernel(
         divide_bias()
         shift_of(0)
         normalise(0)
+        split_quotients()
         spread_quotients()
         transpose(0)
         front(1)

@@ -33,7 +33,7 @@ BANK = 512
 QK = slice(0, 2 * C)
 V = slice(2 * C, 3 * C)
 S_EXTRA = ()
-VECTOR_UNITS = 3
+VECTOR_UNITS = 4
 SCALAR_UNITS = 2
 W_ENGINES = "GGGGGG"
 
@@ -62,15 +62,16 @@ def tile_swidtblock_pa_t_kernel(
         ctx.enter_context(tc.manual_schedule(engines={mybir.EngineType.DVE}))
 
         x_tiles = []
-
-        def load_x(s, parts):
+        for s in range(GROUPS):
             x_sb = xpool.tile([P, A, D], BF16)
-            step = A // parts
-            for a in range(0, A, step):
-                nc.sync.dma_start(out=x_sb[:, a : a + step], in_=x_groups[s, :, a : a + step])
             x_tiles.append(x_sb)
 
-        load_x(0, A)
+        def load_x(s, first, count):
+            tiles = slice(first, first + count)
+            nc.sync.dma_start(out=x_tiles[s][:, tiles], in_=x_groups[s, :, tiles])
+
+        for a in range(A):
+            load_x(0, a, 1)
         w_raw = const.tile([P, 3, PASSES, PACK, C], BF16)
 
         def load_w(o):
@@ -79,11 +80,14 @@ def tile_swidtblock_pa_t_kernel(
             )
 
         load_w(0)
-        load_x(1, 2)
+        for i in range(2):
+            load_x(1, T2 * i, T2)
+        load_x(2, 0, T2)
         load_w(1)
         load_w(2)
-        for s in range(2, GROUPS):
-            load_x(s, 1)
+        load_x(2, T2, T2)
+        for s in range(3, GROUPS):
+            load_x(s, 0, A)
 
         eps = const.tile([P, 1], F32)
         nc.vector.memset(eps[:], EPS)
@@ -114,10 +118,7 @@ def tile_swidtblock_pa_t_kernel(
         out_bias_v = const.tile([P, 2, C], F32)
 
         def divide_bias():
-            nc.vector.tensor_scalar(
-                out=size[:], in0=gain_raw[:], scalar1=-1.0, scalar2=0.0, op0=ALU.mult, op1=ALU.add
-            )
-            nc.vector.tensor_tensor(out=size[:], in0=size[:], in1=gain_raw[:], op=ALU.max)
+            nc.scalar.activation(out=size[:], in_=gain_raw[:], func=ACT.Abs)
             nc.vector.tensor_scalar(
                 out=size[:], in0=size[:], scalar1=TINY, scalar2=TINY, op0=ALU.is_lt, op1=ALU.mult
             )
@@ -168,13 +169,16 @@ def tile_swidtblock_pa_t_kernel(
             for i in range(2):
                 nc.scalar.copy(out=out_bias_v[:, i], in_=spread_v[:, 0:C])
 
-        w_grouped = const.tile([P, PASSES, 3 * C, PACK], BF16, align_bytes=64)
-        w_codes = const.tile([P, PASSES, 3 * C], U32, align_bytes=64)
-        w_scales = const.tile([P, PASSES, 3 * C], U8, align_bytes=64)
+        w_grouped_qk = const.tile([P, PASSES, 2 * C, PACK], BF16, align_bytes=64)
+        w_grouped_v = const.tile([P, PASSES, C, PACK], BF16, align_bytes=64)
+        w_codes_qk = const.tile([P, PASSES, 2 * C], U32, align_bytes=64)
+        w_codes_v = const.tile([P, PASSES, C], U32, align_bytes=64)
+        w_scales_qk = const.tile([P, PASSES, 2 * C], U8, align_bytes=64)
+        w_scales_v = const.tile([P, PASSES, C], U8, align_bytes=64)
 
         def regroup_weight(o):
             for g in range(PASSES):
-                dst = w_grouped[:, g, o * C : (o + 1) * C, :]
+                dst = w_grouped_qk[:, g, o * C : (o + 1) * C] if o < 2 else w_grouped_v[:, g]
                 src = w_raw[:, o, g].rearrange("p j c -> p c j")
                 if W_ENGINES[2 * o + g] == "S":
                     nc.scalar.copy(out=dst, in_=src)
@@ -186,13 +190,14 @@ def tile_swidtblock_pa_t_kernel(
                     )
 
         def quantise_weights():
-            for g in range(PASSES):
-                for cols in (QK, V):
-                    nc.vector.quantize_mx(
-                        out=w_codes[:, g, cols].bitcast(FP8X4),
-                        scales=w_scales[:, g, cols],
-                        in_=w_grouped[:, g, cols, :].rearrange("p c j -> p (c j)"),
-                    )
+            for grouped, codes, scales in (
+                (w_grouped_qk, w_codes_qk, w_scales_qk), (w_grouped_v, w_codes_v, w_scales_v),
+            ):
+                nc.vector.quantize_mx(
+                    out=codes[:].rearrange("p g c -> p (g c)").bitcast(FP8X4),
+                    scales=scales[:].rearrange("p g c -> p (g c)"),
+                    in_=grouped[:].rearrange("p g c j -> p (g c j)"),
+                )
 
         mean_tiles = {}
         rstd_tiles = {}
@@ -379,13 +384,15 @@ def tile_swidtblock_pa_t_kernel(
                 acc_tiles[i].append(acc_qk)
                 qk_out = acc_qk[:].rearrange("p o c -> p (o c)")
                 for g in range(PASSES):
-                    for out, cols in ((qk_out, QK), (acc_v[:, b], V)):
+                    for out, w_codes, w_scales in (
+                        (qk_out, w_codes_qk, w_scales_qk), (acc_v[:, b], w_codes_v, w_scales_v),
+                    ):
                         nc.tensor.matmul_mx(
                             out=out,
                             lhsT=codes[:, g, tokens].bitcast(FP8X4),
                             lhsT_scale=scales[:, g, tokens],
-                            rhs=w_codes[:, g, cols].bitcast(FP8X4),
-                            rhs_scale=w_scales[:, g, cols],
+                            rhs=w_codes[:, g].bitcast(FP8X4),
+                            rhs_scale=w_scales[:, g],
                             start=(g == 0),
                             stop=(g == PASSES - 1),
                         )
@@ -435,16 +442,16 @@ def tile_swidtblock_pa_t_kernel(
         front(1)
         deviation(1)
         regroup_weight(0)
-        shift_of(1)
-        normalise(1)
-        regroup_weight(1)
-        regroup_weight(2)
         front(2)
         deviation(2)
+        shift_of(1)
+        normalise(1)
         scale(0)
         shift_of(2)
         normalise(2)
         transpose(1)
+        regroup_weight(1)
+        regroup_weight(2)
         front(3)
         deviation(3)
         spread_vectors()

from contextlib import ExitStack

import concourse.mybir as mybir
from concourse.masks import make_identity

F32 = mybir.dt.float32
BF16 = mybir.dt.bfloat16
U32 = mybir.dt.uint32
U8 = mybir.dt.uint8
FP8X4 = mybir.dt.float8_e4m3fn_x4
ALU = mybir.AluOpType
ACT = mybir.ActivationFunctionType

P = 128
PACK = 4
K_PASS = P * PACK
TOKENS = 4 * 1024
D = 1024
C = 256
EPS = 1e-6
TINY = 2.0**-60

PASSES = D // K_PASS
SLOTS = PASSES * PACK
A = 4
GROUP = A * P
GROUPS = TOKENS // GROUP
T2 = 2
UNIT = T2 * P
UNITS = TOKENS // UNIT
BN_MAX = 512
BANK = 512
QK = slice(0, 2 * C)
V = slice(2 * C, 3 * C)
S_EXTRA = ()
VECTOR_UNITS = 4
SCALAR_UNITS = 2
W_ENGINES = "GGGGGG"

FLOPS = 2 * TOKENS * D * 3 * C


def tile_swidtblock_pa_t_kernel(
    tc, x, ln1_gain, ln1_bias, wq, bq, wk, bk, wv, bv, out_0, out_1, out_2
):
    nc = tc.nc
    x_groups = x.flatten_outer_dims().rearrange("(s p a) d -> s p a d", p=P, a=A)
    out_groups = [
        o.rearrange("b t h e -> (b t) (h e)").rearrange("(s p a) c -> s p a c", p=P, a=A)
        for o in (out_0, out_1, out_2)
    ]

    with ExitStack() as ctx:
        const = ctx.enter_context(tc.tile_pool(name="const", bufs=1))
        xpool = ctx.enter_context(tc.tile_pool(name="xpool", bufs=GROUPS))
        small = ctx.enter_context(tc.tile_pool(name="small", bufs=8))
        work2 = ctx.enter_context(tc.tile_pool(name="work2", bufs=2))
        work3 = ctx.enter_context(tc.tile_pool(name="work3", bufs=3))
        work4 = ctx.enter_context(tc.tile_pool(name="work4", bufs=4))
        psum = ctx.enter_context(tc.psum_pool(name="psum", bufs=4))

        ctx.enter_context(tc.manual_schedule(engines={mybir.EngineType.DVE}))

        x_tiles = []
        for s in range(GROUPS):
            x_sb = xpool.tile([P, A, D], BF16)
            x_tiles.append(x_sb)

        def load_x(s, first, count):
            tiles = slice(first, first + count)
            nc.sync.dma_start(out=x_tiles[s][:, tiles], in_=x_groups[s, :, tiles])

        for a in range(A):
            load_x(0, a, 1)
        w_raw = const.tile([P, 3, PASSES, PACK, C], BF16)

        def load_w(o):
            nc.sync.dma_start(
                out=w_raw[:, o], in_=(wq, wk, wv)[o].rearrange("(g p j) c -> p g j c", j=PACK, p=P)
            )

        load_w(0)
        for i in range(2):
            load_x(1, T2 * i, T2)
        load_x(2, 0, T2)
        load_w(1)
        load_w(2)
        load_x(2, T2, T2)
        for s in range(3, GROUPS):
            load_x(s, 0, A)

        eps = const.tile([P, 1], F32)
        nc.vector.memset(eps[:], EPS)
        warm = const.tile([P, 1], F32)
        nc.scalar.activation(
            out=warm[:], in_=eps[:], func=ACT.Abs_reciprocal_sqrt, bias=eps[:, 0:1], scale=1.0
        )
        gain_raw = const.tile([P, PASSES, PACK], BF16)
        bias_raw = const.tile([P, PASSES, PACK], BF16)
        bias = const.tile([P, PASSES, PACK], F32)
        for raw, vec in ((gain_raw, ln1_gain), (bias_raw, ln1_bias)):
            nc.scalar.dma_start(out=raw[:], in_=vec.rearrange("(g p j) -> p g j", p=P, j=PACK))
        bias_rows = const.tile([P, 3 * C], BF16)
        nc.gpsimd.memset(bias_rows[:], 0.0)
        for o, b in enumerate((bq, bk, bv)):
            nc.scalar.dma_start(
                out=bias_rows[0:1, o * C : (o + 1) * C], in_=b.rearrange("(r c) -> r c", r=1)
            )
        ident = const.tile([P, P], F32)
        make_identity(nc, ident[:])
        ones = const.tile([P, P], BF16)
        nc.gpsimd.memset(ones[:], 1.0)
        gain = const.tile([P, PASSES, PACK], F32)
        size = const.tile([P, PASSES, PACK], F32)
        quotient = const.tile([P, PASSES, PACK], F32)
        quotients = const.tile([P, PASSES, PACK, P], F32)
        out_bias_qk = const.tile([P, 2, C], F32)
        out_bias_v = const.tile([P, 2, C], F32)

        def divide_bias():
            nc.scalar.activation(out=size[:], in_=gain_raw[:], func=ACT.Abs)
            nc.vector.tensor_scalar(
                out=size[:], in0=size[:], scalar1=TINY, scalar2=TINY, op0=ALU.is_lt, op1=ALU.mult
            )
            nc.vector.tensor_tensor(out=gain[:], in0=size[:], in1=gain_raw[:], op=ALU.add)
            nc.scalar.copy(out=bias[:], in_=bias_raw[:])
            nc.vector.reciprocal(out=size[:], in_=gain[:])
            nc.vector.tensor_tensor(out=quotient[:], in0=size[:], in1=bias_raw[:], op=ALU.mult)

        parts = const.tile([P, PACK, P // PACK], F32)
        nc.gpsimd.memset(parts[:], 0.0)
        rest = const.tile([P, PACK], F32)
        rounded = const.tile([P, 2, PACK], BF16)
        parts_by_row = const.tile([P, P], BF16)
        selector = const.tile([P, PACK, P], BF16)
        nc.gpsimd.memset(selector[:], 0.0)
        for j in range(PACK):
            nc.gpsimd.memset(selector[32 * j : 32 * (j + 1), j], 1.0)

        def split_quotients():
            left = quotient[:, 0]
            for i in range(2):
                nc.scalar.copy(out=rounded[:, i], in_=left)
                nc.scalar.copy(out=parts[:, :, i], in_=rounded[:, i])
                out = rest[:] if i == 0 else parts[:, :, 2]
                nc.vector.tensor_tensor(out=out, in0=left, in1=rounded[:, i], op=ALU.subtract)
                left = rest[:]
            bank = psum.tile([P, PACK, P], F32, tag="bank")
            nc.tensor.transpose(bank[:, 0], parts[:].rearrange("p j i -> p (j i)"), ident[:])
            nc.scalar.copy(out=parts_by_row[:], in_=bank[:, 0])

        def spread_quotients():
            for g in range(1, PASSES):
                bank = psum.tile([P, PACK, P], F32, tag="bank")
                for j in range(PACK):
                    nc.tensor.transpose(
                        bank[:, j], quotient[:, g, j : j + 1].to_broadcast([P, P]), ident[:]
                    )
                nc.scalar.copy(out=quotients[:, g], in_=bank[:])

        def spread_vectors():
            spread_qk = psum.tile([P, BANK], F32, tag="bank")
            spread_v = psum.tile([P, BANK], F32, tag="bank")
            for bank, cols, width in ((spread_qk, QK, 2 * C), (spread_v, V, C)):
                nc.tensor.matmul(
                    bank[:, 0:width], lhsT=ones[:], rhs=bias_rows[:, cols], start=True, stop=True
                )
            nc.scalar.copy(out=out_bias_qk[:].rearrange("p o c -> p (o c)"), in_=spread_qk[:])
            for i in range(2):
                nc.scalar.copy(out=out_bias_v[:, i], in_=spread_v[:, 0:C])

        w_grouped_qk = const.tile([P, PASSES, 2 * C, PACK], BF16, align_bytes=64)
        w_grouped_v = const.tile([P, PASSES, C, PACK], BF16, align_bytes=64)
        w_codes_qk = const.tile([P, PASSES, 2 * C], U32, align_bytes=64)
        w_codes_v = const.tile([P, PASSES, C], U32, align_bytes=64)
        w_scales_qk = const.tile([P, PASSES, 2 * C], U8, align_bytes=64)
        w_scales_v = const.tile([P, PASSES, C], U8, align_bytes=64)

        def regroup_weight(o):
            for g in range(PASSES):
                dst = w_grouped_qk[:, g, o * C : (o + 1) * C] if o < 2 else w_grouped_v[:, g]
                src = w_raw[:, o, g].rearrange("p j c -> p c j")
                if W_ENGINES[2 * o + g] == "S":
                    nc.scalar.copy(out=dst, in_=src)
                elif W_ENGINES[2 * o + g] == "V":
                    nc.vector.tensor_copy(out=dst, in_=src)
                else:
                    nc.gpsimd.tensor_scalar(
                        out=dst, in0=src, scalar1=1.0, scalar2=0.0, op0=ALU.mult, op1=ALU.add
                    )

        def quantise_weights():
            for grouped, codes, scales in (
                (w_grouped_qk, w_codes_qk, w_scales_qk), (w_grouped_v, w_codes_v, w_scales_v),
            ):
                nc.vector.quantize_mx(
                    out=codes[:].rearrange("p g c -> p (g c)").bitcast(FP8X4),
                    scales=scales[:].rearrange("p g c -> p (g c)"),
                    in_=grouped[:].rearrange("p g c j -> p (g c j)"),
                )

        mean_tiles = {}
        rstd_tiles = {}
        n_tiles = {}
        bank_tiles = {}
        grouped_tiles = {}
        code_tiles = {}
        acc_tiles = {}
        result_tiles = {}

        def x_of(i, b):
            return x_tiles[i // 2][:, T2 * (i % 2) + b, :]

        def vector_statistics(i):
            mean_var = small.tile([P, T2, 2], F32)
            mean_tiles[i] = mean_var
            stats = [None] * T2
            for b in range(T2):
                if (i, b) in S_EXTRA:
                    scalar_tile(i, b)
                    continue
                pair = small.tile([P, D // BN_MAX, 6], F32)
                stats[b] = pair
                for half in range(D // BN_MAX):
                    nc.vector.bn_stats(
                        out=pair[:, half, :], in_=x_of(i, b)[:, half * BN_MAX : (half + 1) * BN_MAX]
                    )
            for b in range(T2):
                if (i, b) in S_EXTRA:
                    continue
                nc.vector.bn_aggr(
                    out=mean_var[:, b, :], in_=stats[b][:].rearrange("p h s -> p (h s)")
                )

        def scalar_tile(i, b):
            mean_var = mean_tiles[i]
            unread = work2.tile([P, D], BF16)
            squares = small.tile([P, 1], F32)
            nc.scalar.activation(
                out=unread[:], in_=x_of(i, b), func=ACT.Identity, scale=1.0 / D,
                accum_out=mean_var[:, b, 0:1],
            )
            nc.scalar.activation(
                out=unread[:], in_=x_of(i, b), func=ACT.Square, scale=-1.0,
                bias=mean_var[:, b, 0:1], accum_out=squares[:],
            )
            nc.scalar.activation(
                out=mean_var[:, b, 1:2], in_=squares[:], func=ACT.Copy, scale=1.0 / D
            )

        def scalar_statistics(i):
            mean_squares = small.tile([P, T2, 2], F32)
            mean_tiles[i] = mean_squares
            unread = work2.tile([P, D], BF16)
            for b in range(T2):
                nc.scalar.activation(
                    out=unread[:], in_=x_of(i, b), func=ACT.Identity, scale=-1.0 / D,
                    accum_out=mean_squares[:, b, 0:1],
                )
            for b in range(T2):
                nc.scalar.activation(
                    out=unread[:], in_=x_of(i, b), func=ACT.Square, scale=1.0,
                    bias=mean_squares[:, b, 0:1], accum_out=mean_squares[:, b, 1:2],
                )

        def deviation(i):
            rstd = small.tile([P, T2], F32)
            shift = small.tile([P, T2], F32)
            rstd_tiles[i] = (rstd, shift)
            nc.scalar.activation(
                out=rstd[:], in_=mean_tiles[i][:, :, 1], func=ACT.Abs_reciprocal_sqrt,
                bias=eps[:, 0:1], scale=1.0 if i < VECTOR_UNITS else 1.0 / D,
            )

        def shift_of(i):
            rstd, shift = rstd_tiles[i]
            nc.vector.scalar_tensor_tensor(
                out=shift[:], in0=mean_tiles[i][:, :, 0], scalar=-1.0 if i < VECTOR_UNITS else 1.0,
                in1=rstd[:], op0=ALU.mult, op1=ALU.mult,
            )

        def normalise(i):
            n_sb = work4.tile([P, T2, PASSES, PACK, P], F32)
            n_tiles[i] = n_sb
            rstd, shift = rstd_tiles[i]
            engine = nc.vector if i < 1 else nc.gpsimd
            for b in range(T2):
                engine.tensor_scalar(
                    out=n_sb[:, b], in0=x_of(i, b).rearrange("q (g p j) -> q g j p", j=PACK, p=P),
                    scalar1=rstd[:, b : b + 1], scalar2=shift[:, b : b + 1],
                    op0=ALU.mult, op1=ALU.add,
                )

        def transpose_alone(i):
            n_sb = n_tiles[i]
            for g in range(PASSES):
                for half in range(2):
                    bank = psum.tile([P, 2, UNIT], F32, tag="bank")
                    bank_tiles[(i, g, half)] = bank
                    for jj in range(2):
                        for b in range(T2):
                            nc.tensor.transpose(
                                bank[:, jj, b * P : (b + 1) * P], n_sb[:, b, g, 2 * half + jj],
                                ident[:],
                            )

        def scale_on_scalar(i):
            grouped = work2.tile([P, PASSES, UNIT, PACK], BF16, align_bytes=64)
            grouped_tiles[i] = grouped
            for g in range(PASSES):
                h_t = work2.tile([P, PACK, UNIT], BF16)
                for j in range(PACK):
                    nc.scalar.activation(
                        out=h_t[:, j], in_=bank_tiles[(i, g, j // 2)][:, j % 2], func=ACT.Identity,
                        scale=gain[:, g, j : j + 1], bias=bias[:, g, j : j + 1],
                    )
                nc.gpsimd.tensor_scalar(
                    out=grouped[:, g], in0=h_t[:].rearrange("p j c -> p c j"),
                    scalar1=1.0, scalar2=0.0, op0=ALU.mult, op1=ALU.add,
                )

        def transpose(i):
            if i in (14, 15):
                transpose_alone(i)
                return
            n_sb = n_tiles[i]
            for b in range(T2):
                for g in range(PASSES):
                    bank = psum.tile([P, PACK, P], F32, tag="bank")
                    bank_tiles[(i, b, g)] = bank
                    if g == 0:
                        nc.tensor.matmul(
                            bank[:].rearrange("p j n -> p (j n)"), lhsT=parts_by_row[:],
                            rhs=selector[:].rearrange("p j n -> p (j n)"), start=True, stop=False,
                        )
                        for j in range(PACK):
                            nc.tensor.matmul(
                                bank[:, j], lhsT=n_sb[:, b, g, j], rhs=ident[:], is_transpose=True,
                                start=False, stop=(j == PACK - 1),
                            )
                        continue
                    for j in range(PACK):
                        nc.tensor.matmul(
                            bank[:, j], lhsT=n_sb[:, b, g, j], rhs=ident[:], is_transpose=True,
                            start=True, stop=False,
                        )
                        nc.tensor.matmul(
                            bank[:, j], lhsT=quotients[:, g, j], rhs=ident[:], is_transpose=True,
                            start=False, stop=True,
                        )

        def scale(i):
            if i in (14, 15):
                scale_on_scalar(i)
                return
            grouped = work2.tile([P, PASSES, UNIT, PACK], BF16, align_bytes=64)
            grouped_tiles[i] = grouped
            for b in range(T2):
                for g in range(PASSES):
                    nc.vector.tensor_tensor(
                        out=grouped[:, g, b * P : (b + 1) * P, :],
                        in0=bank_tiles[(i, b, g)][:].rearrange("p j n -> p n j"),
                        in1=gain[:, g].unsqueeze(1).to_broadcast([P, P, PACK]),
                        op=ALU.mult,
                    )

        def quantise(i):
            codes = work3.tile([P, PASSES, UNIT], U32, align_bytes=64)
            scales = work3.tile([P, PASSES, UNIT], U8, align_bytes=64)
            code_tiles[i] = (codes, scales)
            nc.vector.quantize_mx(
                out=codes[:].rearrange("p g n -> p (g n)").bitcast(FP8X4),
                scales=scales[:].rearrange("p g n -> p (g n)"),
                in_=grouped_tiles[i][:].rearrange("p g n j -> p (g n j)"),
            )

        def multiply(i):
            codes, scales = code_tiles[i]
            acc_v = psum.tile([P, T2, C], F32, tag="product")
            acc_tiles[i] = [acc_v]
            for b in range(T2):
                tokens = slice(b * P, (b + 1) * P)
                acc_qk = psum.tile([P, 2, C], F32, tag="product")
                acc_tiles[i].append(acc_qk)
                qk_out = acc_qk[:].rearrange("p o c -> p (o c)")
                for g in range(PASSES):
                    for out, w_codes, w_scales in (
                        (qk_out, w_codes_qk, w_scales_qk), (acc_v[:, b], w_codes_v, w_scales_v),
                    ):
                        nc.tensor.matmul_mx(
                            out=out,
                            lhsT=codes[:, g, tokens].bitcast(FP8X4),
                            lhsT_scale=scales[:, g, tokens],
                            rhs=w_codes[:, g].bitcast(FP8X4),
                            rhs_scale=w_scales[:, g],
                            start=(g == 0),
                            stop=(g == PASSES - 1),
                        )

        def add_bias(i):
            result = work4.tile([P, 3, T2, C], F32)
            result_tiles[i] = result
            acc_v, *acc_qk = acc_tiles[i]
            for b in range(T2):
                nc.vector.tensor_tensor(
                    out=result[:, 0:2, b, :], in0=acc_qk[b][:], in1=out_bias_qk[:], op=ALU.add
                )
            nc.vector.tensor_tensor(
                out=result[:, 2], in0=acc_v[:], in1=out_bias_v[:], op=ALU.add
            )

        def store(i):
            a = T2 * (i % 2)
            for o in range(3):
                nc.sync.dma_start(
                    out=out_groups[o][i // 2, :, a : a + T2], in_=result_tiles[i][:, o]
                )

        def stage(function, i):
            if 0 <= i < UNITS:
                function(i)

        def scalar_front(i):
            if i >= VECTOR_UNITS:
                scalar_statistics(i)
                deviation(i)

        def front(i):
            if i < VECTOR_UNITS:
                vector_statistics(i)
            else:
                scalar_statistics(i)

        front(0)
        deviation(0)
        divide_bias()
        shift_of(0)
        normalise(0)
        split_quotients()
        spread_quotients()
        transpose(0)
        front(1)
        deviation(1)
        regroup_weight(0)
        front(2)
        deviation(2)
        shift_of(1)
        normalise(1)
        scale(0)
        shift_of(2)
        normalise(2)
        transpose(1)
        regroup_weight(1)
        regroup_weight(2)
        front(3)
        deviation(3)
        spread_vectors()
        quantise(0)
        front(4)
        scale(1)
        shift_of(3)
        normalise(3)
        quantise_weights()
        transpose(2)
        quantise(1)
        for u in range(2, UNITS + 3):
            stage(front, u + 3)
            stage(deviation, u + 2)
            stage(shift_of, u + 2)
            stage(normalise, u + 2)
            stage(scale, u)
            stage(multiply, u - 2)
            stage(transpose, u + 1)
            stage(add_bias, u - 2)
            stage(store, u - 2)
            stage(quantise, u)
